import numpy as np
import ml_dtypes


def mxq(x, axis, fmt="e4m3"):
    dtype, down = {"e4m3": (ml_dtypes.float8_e4m3fn, 7), "e5m2": (ml_dtypes.float8_e5m2, 14)}[fmt]
    v = np.moveaxis(np.asarray(x, np.float32).astype(ml_dtypes.bfloat16).astype(np.float64), axis, -1)
    blocks = v.reshape(v.shape[:-1] + (-1, 32))
    amax = np.abs(blocks).max(-1, keepdims=True)
    byte = np.maximum(np.where(amax > 0, np.frexp(amax)[1] - 1 + 127, 0) - down, 1)
    scale = np.exp2(byte - 127.0)
    codes = (blocks / scale).astype(np.float32).astype(dtype).astype(np.float64)
    return np.moveaxis((codes * scale).reshape(v.shape), -1, axis)


WIDE = False


def mx_kscale(k):
    if not WIDE:
        return np.ones(k)
    levels = np.array([10, -10, 5, -5, 0])
    if k % 512:
        return np.exp2(np.random.permutation(np.resize(levels, k // 32))).repeat(32)
    a = np.empty((k // 512, 16))
    for p in range(k // 512):
        a[p, :8] = np.random.permutation(np.resize(levels, 8))
        for g in range(8):
            far = levels[np.abs(levels - a[p, g]) >= 10]
            a[p, g + 8] = far[np.random.randint(len(far))]
    return np.exp2(a.ravel()).repeat(32)


BF16 = ml_dtypes.bfloat16


def bf(x):
    return np.asarray(x, np.float32).astype(BF16)


def f64(x):
    return np.asarray(x).astype(np.float64)


E2M1 = np.array([0.0, 0.5, 1.0, 1.5, 2.0, 3.0, 4.0, 6.0, -0.0, -0.5, -1.0, -1.5, -2.0, -3.0, -4.0, -6.0])


def pack_weight(w, fmt):
    k, n = w.shape
    w = f64(bf(w)).reshape(k // 32, 32, n)
    amax = np.abs(w).max(1)
    if fmt == "e4m3":
        byte = np.frexp(amax)[1] - 1 + 127 - 7
    else:
        mant, ex = np.frexp(amax / 6.0)
        byte = np.where(mant > 0.5, ex, ex - 1) + 127
    byte = np.clip(np.where(amax > 0, byte, 1), 1, 254)
    scaled = (w * np.exp2(127.0 - byte)[:, None, :]).reshape(k, n).astype(np.float32)
    by_word = np.ascontiguousarray(scaled.reshape(k // 512, 128, 4, n).transpose(0, 1, 3, 2))
    if fmt == "e4m3":
        words = by_word.astype(ml_dtypes.float8_e4m3fn).view(np.uint8)
    else:
        c = by_word.astype(ml_dtypes.float4_e2m1fn).view(np.uint8) & 0xF
        words = c[..., 0::2] | (c[..., 1::2] << 4)
    return np.ascontiguousarray(words), np.ascontiguousarray(byte.astype(np.uint8).reshape(k // 512, 16, n))


def unpack_weight(words, scales, fmt):
    g, p, n, _ = words.shape
    if fmt == "e4m3":
        vals = np.ascontiguousarray(words).view(ml_dtypes.float8_e4m3fn).astype(np.float64)
    else:
        nib = np.empty((g, p, n, 4), np.uint8)
        nib[..., 0::2] = words & 0xF
        nib[..., 1::2] = words >> 4
        vals = E2M1[nib]
    vals = vals * np.repeat(np.exp2(scales.astype(np.float64) - 127.0), 8, axis=1)[..., None]
    return vals.transpose(0, 1, 3, 2).reshape(g * 512, n)


N, T, B, C, H = 256, 4, 8, 512, 128
N3 = T * N
O = H + H


def sigmoid(v):
    return 1.0 / (1.0 + np.exp(-v))


def draw0():
    s, t = mx_kscale(N3), mx_kscale(C)
    x = bf(np.random.standard_normal((N3, B, C)) * s[:, None, None] * t[None, None, :])
    A = bf(np.random.standard_normal((N3, N3)) / np.sqrt(N3) / s[None, :])
    W0 = np.random.standard_normal((O, C)) / np.sqrt(C) / t[None, :]
    words, scales = pack_weight(W0.T, "e4m3")
    return {"x": x,
            "A": A,
            "W0_words": words,
            "W0_scales": scales,
            "b0": bf(np.random.standard_normal(O) * 0.3)}


def core(x, A, W0_words, W0_scales, b0):
    h = f64(x).transpose(1, 2, 0)
    g = mxq(h, 2, "e4m3") @ mxq(f64(A), 1, "e4m3").T
    y = (unpack_weight(W0_words, W0_scales, "e4m3").T @ mxq(g, 1, "e4m3")) + f64(b0)[None, :, None]
    h1 = y[:, :H] * sigmoid(y[:, H:])
    return h1.transpose(2, 0, 1)


def e4m3fn_bytes(y):
    return np.clip(np.asarray(y, np.float64), -448.0, 448.0).astype(np.float32).astype(ml_dtypes.float8_e4m3fn).view(np.uint8)


def e4m3fn_values(b):
    return np.asarray(b, np.uint8).view(ml_dtypes.float8_e4m3fn).astype(np.float64)


def setup_inputs():
    d = draw0()
    x0 = np.asarray(d['A']).astype(np.float64)
    s = (np.max(np.abs(x0), axis=(0,), keepdims=True) / 448.0).astype(np.float32)
    out = {}
    for k, v in d.items():
        if k == 'A':
            out['A_bytes'] = e4m3fn_bytes(x0 / s.astype(np.float64))
            out['A_scale'] = s
        else:
            out[k] = v
    return out


def reference(x, A_bytes, A_scale, W0_words, W0_scales, b0):
    return core(x, e4m3fn_values(A_bytes) * A_scale.astype(np.float64), W0_words, W0_scales, b0)

@@ -1,0 +1,239 @@
+from contextlib import ExitStack
+
+import concourse.mybir as mybir
+from concourse.masks import make_identity
+
+F32 = mybir.dt.float32
+BF16 = mybir.dt.bfloat16
+I32 = mybir.dt.int32
+U32 = mybir.dt.uint32
+U8 = mybir.dt.uint8
+FP8 = mybir.dt.float8_e4m3fn
+FP8X4 = mybir.dt.float8_e4m3fn_x4
+MULT = mybir.AluOpType.mult
+ADD = mybir.AluOpType.add
+ACT = mybir.ActivationFunctionType
+
+NODES, BATCH, CHAN, HID = 1024, 8, 512, 128
+P = 128
+VT = NODES // P
+FLOPS = 2 * NODES * NODES * BATCH * CHAN + 2 * NODES * BATCH * CHAN * 2 * HID
+
+
+ORDER = (
+    "il 0 0 2, prod 0, il 0 1 0, prod 1, tra 0, il 0 1 1, prod 2, tra 1, eva 0, qx 0, eva 1, tra 2, "
+    "il 1 0 0, qa 0, qa 1, mm1 0 0, prod 3, eva 2, mm1 0 1, evg 0 0, qa 2, tra 3, il 1 0 1, evg 0 1, "
+    "mm1 0 2, eva 3, prod 4, evg 0 2, qa 3, tra 4, il 1 1 2, mm1 0 3, eva 4, evg 0 3, qa 4, qx 1, "
+    "mm1 0 4, evg 0 4, qg 0 0, mm1 1 0, prod 5, mm2 0 0, evg 1 0, mm1 1 1, sig 0 0, prod 6, mm1 1 2, evg 1 1, "
+    "mm1 1 3, evg 1 2, glu 0 0, mm1 1 4, evg 1 3, il 2 0 0, tra 5, evg 1 4, qg 1 0, tra 6, eva 5, il 2 0 1, "
+    "mm2 1 0, eva 6, qa 5, tro 0 0, prod 7, sig 1 0, mm1 0 5, evo 0 0, mm1 1 5, glu 1 0, evg 0 5, qa 6, "
+    "tra 7, evg 1 5, il 2 1 2, mm1 0 6, eva 7, mm1 1 6, evg 0 6, qa 7, tro 1 0, qx 2, evg 1 6, mm1 0 7, "
+    "evo 1 0, mm1 1 7, il 3 0 2, evg 0 7, mm1 2 0, evg 1 7, mm1 2 1, evg 2 0, qg 0 1, mm1 2 2, evg 2 1, qg 1 1, "
+    "mm2 0 1, il 3 1 2, evg 2 2, mm1 2 3, sig 0 1, mm1 2 4, evg 2 3, glu 0 1, mm1 2 5, evg 2 4, qx 3, mm2 1 1, "
+    "evg 2 5, mm1 2 6, sig 1 1, qg 2 0, mm1 2 7, evg 2 6, glu 1 1, mm1 3 0, evg 2 7, il 4 0 0, mm2 2 0, evg 3 0, "
+    "qg 2 1, mm1 3 1, sig 2 0, il 4 0 1, mm1 3 2, evg 3 1, glu 2 0, mm1 3 3, evg 3 2, il 4 1 2, mm2 2 1, evg 3 3, "
+    "mm1 3 4, sig 2 1, mm1 3 5, qg 3 0, evg 3 4, mm1 3 6, glu 2 1, evg 3 5, mm1 3 7, qx 4, evg 3 6, mm2 3 0, "
+    "evg 3 7, tro 0 1, il 5 0 0, sig 3 0, mm1 4 0, qg 3 1, mm1 4 1, glu 3 0, evg 4 0, mm1 4 2, il 5 0 1, evg 4 1, "
+    "mm2 3 1, evg 4 2, il 5 1 2, mm1 4 3, sig 3 1, mm1 4 4, evg 4 3, glu 3 1, mm1 4 5, evg 4 4, qx 5, mm1 4 6, "
+    "evg 4 5, mm1 4 7, evg 4 6, qg 4 0, tro 1 1, evg 4 7, evo 0 1, mm2 4 0, qg 4 1, mm1 5 0, sig 4 0, evo 1 1, "
+    "mm1 5 1, evg 5 0, glu 4 0, mm1 5 2, evg 5 1, il 6 0 2, mm2 4 1, evg 5 2, mm1 5 3, sig 4 1, il 6 1 0, tro 2 0, "
+    "evg 5 3, mm1 5 4, glu 4 1, evo 2 0, mm1 5 5, qg 5 0, evg 5 4, mm1 5 6, il 6 1 1, evg 5 5, mm2 5 0, il 7 0 0, "
+    "evg 5 6, mm1 5 7, sig 5 0, qx 6, tro 2 1, evg 5 7, tro 3 0, glu 5 0, evo 3 0, mm1 6 0, qg 5 1, mm1 6 1, "
+    "evg 6 0, evo 2 1, mm2 5 1, evg 6 1, il 7 0 1, mm1 6 2, sig 5 1, il 7 1 0, mm1 6 3, evg 6 2, glu 5 1, mm1 6 4, "
+    "evg 6 3, il 7 1 1, mm1 6 5, evg 6 4, qg 6 0, mm1 6 6, evg 6 5, qx 7, mm2 6 0, evg 6 6, mm1 6 7, sig 6 0, "
+    "tro 3 1, evg 6 7, glu 6 0, mm1 7 0, qg 6 1, mm1 7 1, evg 7 0, evo 3 1, mm2 6 1, evg 7 1, mm1 7 2, sig 6 1, "
+    "mm1 7 3, evg 7 2, glu 6 1, tro 4 0, evg 7 3, mm1 7 4, evo 4 0, qg 7 0, mm1 7 5, evg 7 4, mm2 7 0, evg 7 5, "
+    "mm1 7 6, sig 7 0, mm1 7 7, evg 7 6, glu 7 0, tro 4 1, evg 7 7, tro 5 0, evo 4 1, evo 5 0, qg 7 1, tro 5 1, "
+    "tro 6 0, evo 5 1, mm2 7 1, evo 6 0, tro 6 1, sig 7 1, tro 7 0, evo 6 1, evo 7 0, glu 7 1, tro 7 1, evo 7 1, "
+)
+SCALAR_IL = ["0 1 0","0 1 1","1 0 0"]
+
+
+def tile_stsgcm_pa_t_w8_kernel(tc, x, A_bytes, A_scale, W0_words, W0_scales, b0, out):
+    nc = tc.nc
+    with ExitStack() as ctx:
+        const = ctx.enter_context(tc.tile_pool(name="const", bufs=1))
+        raws = ctx.enter_context(tc.tile_pool(name="raws", bufs=1))
+        work = ctx.enter_context(tc.tile_pool(name="work", bufs=3))
+        psg = ctx.enter_context(tc.psum_pool(name="psg", bufs=4))
+        pst = ctx.enter_context(tc.psum_pool(name="pst", bufs=2))
+        psy = ctx.enter_context(tc.psum_pool(name="psy", bufs=1))
+
+        x_view = x.rearrange("(g p j) b c -> g b p j c", p=P, j=4)
+        a_view = A_bytes.rearrange("(k p) w -> p k w", p=P)
+        out_view = out.rearrange("(k p) b j -> b p k j", p=P)
+
+        warm = const.tile([P, 1], F32, name="warm")
+        nc.vector.memset(warm[:], 0.0)
+        nc.scalar.activation(out=warm[:], in_=warm[:], func=ACT.Sigmoid)
+        w_scales = const.tile([P, 2 * HID], U8, name="w_scales", align_bytes=64)
+        nc.vector.memset(w_scales[:].bitcast(I32), 0)
+
+        ident = const.tile([P, P], F32, name="ident")
+        make_identity(nc, ident[:])
+
+        scale_bc = const.tile([P, NODES], F32, name="scale_bc")
+        nc.scalar.dma_start(out=scale_bc[:], in_=A_scale.rearrange("o k -> (o k)").partition_broadcast(P))
+
+        raw = {}
+        a_raw = {}
+
+        def load_x(b, g):
+            t = raws.tile([P, 4, CHAN], BF16, name="raw%d_%d" % (b, g))
+            nc.sync.dma_start(out=t[:], in_=x_view[g][b])
+            raw[b, g] = t
+
+        def load_a(lo, hi):
+            t = raws.tile([P, hi - lo, NODES], U8, name="abytes%d" % lo)
+            nc.sync.dma_start(out=t[:], in_=a_view[:, lo:hi, :])
+            for k in range(lo, hi):
+                a_raw[k] = t[:, k - lo, :]
+
+        load_x(0, 0)
+        load_a(0, 2)
+        load_x(0, 1)
+        load_a(2, 5)
+        load_x(1, 0)
+        load_a(5, 8)
+        load_x(1, 1)
+        w_words = const.tile([P, 2 * HID], U32, name="w_words", align_bytes=64)
+        nc.sync.dma_start(out=w_words[:].bitcast(I32), in_=W0_words.rearrange("o p n t -> (o p) (n t)").bitcast(I32))
+        ws_view = W0_scales.rearrange("o q n -> (o q) n").bitcast(I32)
+        for q in range(4):
+            nc.sync.dma_start(out=w_scales[32 * q : 32 * q + 4, :].bitcast(I32), in_=ws_view[4 * q : 4 * q + 4, :])
+        bias = const.tile([P, 2], BF16, name="bias")
+        with nc.allow_non_contiguous_dma(reason="256 bias values, one to a partition and half"):
+            nc.sync.dma_start(out=bias[:], in_=b0.rearrange("(o p) -> p o", p=P))
+        for b in range(2, 8):
+            for g in range(2):
+                load_x(b, g)
+
+        xq, aw, at, aq, xg, acc, gg, gq, yv, yg, sig, hh, tro, ob = ({} for _ in range(14))
+
+        def il(b, g, hf):
+            if b not in xg:
+                xg[b] = work.tile([P, 2, 2048], BF16, name="xg", bufs=3, align_bytes=64)
+            lo, hi = (0, 512) if hf == 2 else (256 * hf, 256 * hf + 256)
+            dst = xg[b][:, g, :].rearrange("p (t c) -> p t c", t=4)[:, :, lo:hi]
+            src = raw[b, g][:, :, lo:hi]
+            eng = nc.scalar.copy if "%d %d %d" % (b, g, hf) in SCALAR_IL else nc.vector.tensor_copy
+            eng(
+                out=dst.rearrange("p t (m i j) -> p m j i t", i=2, j=4),
+                in_=src.rearrange("p j (m i t) -> p m j i t", i=2, t=4),
+            )
+
+        def qx(b):
+            codes = work.tile([P, 2, CHAN], U32, name="xcodes", bufs=4, align_bytes=64)
+            scales = work.tile([P, 2, CHAN], U8, name="xscales", bufs=4, align_bytes=64)
+            nc.vector.quantize_mx(
+                out=codes[:].rearrange("p g c -> p (g c)").bitcast(FP8X4),
+                scales=scales[:].rearrange("p g c -> p (g c)"),
+                in_=xg[b][:].rearrange("p g c -> p (g c)"),
+            )
+            xq[b] = (codes, scales)
+
+        def prod(k):
+            aw[k] = work.tile([P, NODES], BF16, name="aw", bufs=4)
+            nc.vector.tensor_tensor(out=aw[k][:], in0=a_raw[k].bitcast(FP8), in1=scale_bc[:], op=MULT)
+
+        def tra(k):
+            at[k] = pst.tile([P, 4, P], F32, name="pst_t")
+            words = aw[k][:].bitcast(F32)
+            for g in range(2):
+                for u in range(2):
+                    nc.tensor.transpose(at[k][:, 2 * g + u, :], words[:, 256 * g + u : 256 * (g + 1) : 2], ident[:])
+
+        def eva(k):
+            ag = work.tile([P, NODES], BF16, name="ag", bufs=4, align_bytes=64)
+            nc.scalar.copy(
+                out=ag[:].bitcast(F32).rearrange("p (g v u) -> p g v u", g=2, u=2),
+                in_=at[k][:].rearrange("p (g u) v -> p g v u", g=2),
+            )
+            aq[k] = ag
+
+        def qa(k):
+            codes = const.tile([P, 2, P], U32, name="acodes%d" % k, align_bytes=64)
+            scales = const.tile([P, 2, P], U8, name="ascales%d" % k, align_bytes=64)
+            nc.vector.quantize_mx(
+                out=codes[:].rearrange("p g v -> p (g v)").bitcast(FP8X4),
+                scales=scales[:].rearrange("p g v -> p (g v)"),
+                in_=aq[k][:],
+            )
+            aq[k] = (codes, scales)
+
+        def mm1(b, k):
+            acc[b, k] = psg.tile([P, 4, P], F32, name="psg_t")
+            for t in range(4):
+                for g in range(2):
+                    nc.tensor.matmul_mx(
+                        out=acc[b, k][:, t, :],
+                        lhsT=xq[b][0][:, g, P * t : P * (t + 1)].bitcast(FP8X4),
+                        lhsT_scale=xq[b][1][:, g, P * t : P * (t + 1)],
+                        rhs=aq[k][0][:, g, :].bitcast(FP8X4),
+                        rhs_scale=aq[k][1][:, g, :],
+                        start=(g == 0),
+                        stop=(g == 1),
+                    )
+
+        def evg(b, k):
+            h = (b, k // 4)
+            if k % 4 == 0:
+                gg[h] = work.tile([P, 4, P, 4], BF16, name="gg", bufs=4, align_bytes=64)
+            nc.scalar.copy(out=gg[h][:, k % 4, :, :], in_=acc[b, k][:].rearrange("p t v -> p v t"))
+
+        def qg(b, h):
+            codes = work.tile([P, 512], U32, name="gcodes", bufs=4, align_bytes=64)
+            scales = work.tile([P, 512], U8, name="gscales", bufs=4, align_bytes=64)
+            nc.vector.quantize_mx(
+                out=codes[:].bitcast(FP8X4), scales=scales[:], in_=gg[b, h][:].rearrange("p k v t -> p (k v t)")
+            )
+            gq[b, h] = (codes, scales)
+
+        def mm2(b, h):
+            yv[b, h] = psy.tile([P, 512], F32, name="yv")
+            yg[b, h] = psy.tile([P, 512], F32, name="yg")
+            for dst, o in ((yg, 1), (yv, 0)):
+                nc.tensor.matmul_mx(
+                    out=dst[b, h][:],
+                    lhsT=w_words[:, HID * o : HID * (o + 1)].bitcast(FP8X4),
+                    lhsT_scale=w_scales[:, HID * o : HID * (o + 1)],
+                    rhs=gq[b, h][0][:].bitcast(FP8X4),
+                    rhs_scale=gq[b, h][1][:],
+                    start=True,
+                    stop=True,
+                )
+
+        def sigm(b, h):
+            sig[b, h] = work.tile([P, 512], F32, name="sig")
+            nc.scalar.activation(out=sig[b, h][:], in_=yg[b, h][:], func=ACT.Sigmoid, bias=bias[:, 1:2])
+
+        def glu(b, h):
+            hh[b, h] = work.tile([P, 512], F32, name="hh", bufs=7)
+            nc.vector.scalar_tensor_tensor(
+                out=hh[b, h][:], in0=yv[b, h][:], scalar=bias[:, 0:1], in1=sig[b, h][:], op0=ADD, op1=MULT
+            )
+
+        def trout(b, h):
+            tro[b, h] = pst.tile([P, 4, P], F32, name="pst_t")
+            for k in range(4):
+                nc.tensor.transpose(tro[b, h][:, k, :], hh[b, h][:, P * k : P * (k + 1)], ident[:])
+
+        def evo(b, h):
+            ob[b, h] = work.tile([P, 4, P], F32, name="ob", bufs=4)
+            eng = nc.scalar.copy if h == 0 else nc.vector.tensor_copy
+            eng(out=ob[b, h][:], in_=tro[b, h][:])
+            nc.sync.dma_start(out=out_view[b][:, 4 * h : 4 * h + 4, :], in_=ob[b, h][:])
+
+        stages = {
+            "il": il, "qx": qx, "prod": prod, "tra": tra, "eva": eva, "qa": qa, "mm1": mm1, "evg": evg,
+            "qg": qg, "mm2": mm2, "sig": sigm, "glu": glu, "tro": trout, "evo": evo,
+        }
+
+        def do(name, *args):
+            stages[name](*args)
+
+        with tc.manual_schedule():
+            for item in ORDER.split(", "):
+                if item:
+                    words = item.split(" ")
+                    do(words[0], *[int(w) for w in words[1:]])

@@ -20,33 +20,44 @@ VT = NODES // P
 FLOPS = 2 * NODES * NODES * BATCH * CHAN + 2 * NODES * BATCH * CHAN * 2 * HID
 
 
-ORDER = (
-    "il 0 0 2, prod 0, il 0 1 0, prod 1, tra 0, il 0 1 1, prod 2, tra 1, eva 0, qx 0, eva 1, tra 2, "
-    "il 1 0 0, qa 0, qa 1, mm1 0 0, prod 3, eva 2, mm1 0 1, evg 0 0, qa 2, tra 3, il 1 0 1, evg 0 1, "
-    "mm1 0 2, eva 3, prod 4, evg 0 2, qa 3, tra 4, il 1 1 2, mm1 0 3, eva 4, evg 0 3, qa 4, qx 1, "
-    "mm1 0 4, evg 0 4, qg 0 0, mm1 1 0, prod 5, mm2 0 0, evg 1 0, mm1 1 1, sig 0 0, prod 6, mm1 1 2, evg 1 1, "
-    "mm1 1 3, evg 1 2, glu 0 0, mm1 1 4, evg 1 3, il 2 0 0, tra 5, evg 1 4, qg 1 0, tra 6, eva 5, il 2 0 1, "
-    "mm2 1 0, eva 6, qa 5, tro 0 0, prod 7, sig 1 0, mm1 0 5, evo 0 0, mm1 1 5, glu 1 0, evg 0 5, qa 6, "
-    "tra 7, evg 1 5, il 2 1 2, mm1 0 6, eva 7, mm1 1 6, evg 0 6, qa 7, tro 1 0, qx 2, evg 1 6, mm1 0 7, "
-    "evo 1 0, mm1 1 7, il 3 0 2, evg 0 7, mm1 2 0, evg 1 7, mm1 2 1, evg 2 0, qg 0 1, mm1 2 2, evg 2 1, qg 1 1, "
-    "mm2 0 1, il 3 1 2, evg 2 2, mm1 2 3, sig 0 1, mm1 2 4, evg 2 3, glu 0 1, mm1 2 5, evg 2 4, qx 3, mm2 1 1, "
-    "evg 2 5, mm1 2 6, sig 1 1, qg 2 0, mm1 2 7, evg 2 6, glu 1 1, mm1 3 0, evg 2 7, il 4 0 0, mm2 2 0, evg 3 0, "
-    "qg 2 1, mm1 3 1, sig 2 0, il 4 0 1, mm1 3 2, evg 3 1, glu 2 0, mm1 3 3, evg 3 2, il 4 1 2, mm2 2 1, evg 3 3, "
-    "mm1 3 4, sig 2 1, mm1 3 5, qg 3 0, evg 3 4, mm1 3 6, glu 2 1, evg 3 5, mm1 3 7, qx 4, evg 3 6, mm2 3 0, "
-    "evg 3 7, tro 0 1, il 5 0 0, sig 3 0, mm1 4 0, qg 3 1, mm1 4 1, glu 3 0, evg 4 0, mm1 4 2, il 5 0 1, evg 4 1, "
-    "mm2 3 1, evg 4 2, il 5 1 2, mm1 4 3, sig 3 1, mm1 4 4, evg 4 3, glu 3 1, mm1 4 5, evg 4 4, qx 5, mm1 4 6, "
-    "evg 4 5, mm1 4 7, evg 4 6, qg 4 0, tro 1 1, evg 4 7, evo 0 1, mm2 4 0, qg 4 1, mm1 5 0, sig 4 0, evo 1 1, "
-    "mm1 5 1, evg 5 0, glu 4 0, mm1 5 2, evg 5 1, il 6 0 2, mm2 4 1, evg 5 2, mm1 5 3, sig 4 1, il 6 1 0, tro 2 0, "
-    "evg 5 3, mm1 5 4, glu 4 1, evo 2 0, mm1 5 5, qg 5 0, evg 5 4, mm1 5 6, il 6 1 1, evg 5 5, mm2 5 0, il 7 0 0, "
-    "evg 5 6, mm1 5 7, sig 5 0, qx 6, tro 2 1, evg 5 7, tro 3 0, glu 5 0, evo 3 0, mm1 6 0, qg 5 1, mm1 6 1, "
-    "evg 6 0, evo 2 1, mm2 5 1, evg 6 1, il 7 0 1, mm1 6 2, sig 5 1, il 7 1 0, mm1 6 3, evg 6 2, glu 5 1, mm1 6 4, "
-    "evg 6 3, il 7 1 1, mm1 6 5, evg 6 4, qg 6 0, mm1 6 6, evg 6 5, qx 7, mm2 6 0, evg 6 6, mm1 6 7, sig 6 0, "
-    "tro 3 1, evg 6 7, glu 6 0, mm1 7 0, qg 6 1, mm1 7 1, evg 7 0, evo 3 1, mm2 6 1, evg 7 1, mm1 7 2, sig 6 1, "
-    "mm1 7 3, evg 7 2, glu 6 1, tro 4 0, evg 7 3, mm1 7 4, evo 4 0, qg 7 0, mm1 7 5, evg 7 4, mm2 7 0, evg 7 5, "
-    "mm1 7 6, sig 7 0, mm1 7 7, evg 7 6, glu 7 0, tro 4 1, evg 7 7, tro 5 0, evo 4 1, evo 5 0, qg 7 1, tro 5 1, "
-    "tro 6 0, evo 5 1, mm2 7 1, evo 6 0, tro 6 1, sig 7 1, tro 7 0, evo 6 1, evo 7 0, glu 7 1, tro 7 1, evo 7 1, "
-)
-SCALAR_IL = ["0 1 0","0 1 1","1 0 0"]
+SPLIT = True
+IL_SCALAR = {(0,1,1),(1,0,0),(1,0,1),(2,0,0),(2,0,1)}
+def program(do):
+    def il(b, g):
+        if (b, g, 0) in IL_SCALAR:
+            do("il", b, g, 0); do("il", b, g, 1)
+        else:
+            do("il", b, g, 2)
+    do("cast", 0); do("tra", 0); do("cast", 1); do("tra", 1)
+    do("il", 0, 0, 2); do("il",0,1,1); do("eva", 0); do("cast",2); do("tra",2); do("eva", 1); do("cast",3); do("tra",3); do("il", 0, 1, 0); do("qx", 0)
+    do("eva", 2); do("il",1,0,0); do("il",1,0,1); do("eva", 3); do("qa",0); do("il", 1, 1, 2); do("qa",1); do("qa", 2); do("qx", 1); do("qa", 3)
+    do("cast",4); do("mm1",0,0); do("tra",4); do("cast",5); do("tra",5); do("il",2,0,0); do("eva",4); do("mm1",0,1); do("mm1",0,2); do("mm1",0,3)
+    do("evg",0,0); do("cast",6); do("evg",0,1); do("eva",5); do("cast",7); do("evg",0,2); do("evg",0,3); do("mm1",1,0); do("tra",6); do("tra",7); do("qa",4)
+    do("mm1",1,1); do("evg",1,0); do("il",2,0,1); do("qg",0,0); do("eva",6); do("evg",1,1); do("mm1",1,2); do("qa",5); do("evg",1,2); do("mm1",1,3); do("evg",1,3); do("eva",7); do("mm2",0,0); do("qa",6); do("sig",0,0)
+    do("qg",1,0); do("mm1",0,4); do("mm1",1,4); do("evg",0,4); do("glu",0,0); do("qa",7); do("evg",1,4); do("mm1",0,5); do("mm1",1,5); do("evg",0,5); do("il",2,1,2); do("evg",1,5)
+    do("mm2",1,0); do("sig",1,0); do("mm1",0,6); do("mm1",1,6); do("evg",0,6); do("glu",1,0); do("evg",1,6); do("mm1",0,7); do("mm1",1,7); do("qx",2); do("evg",0,7); do("evg",1,7)
+    do("qg",0,4); do("il",3,0,2)
+    for b in range(2, 8):
+        for v in range(4):
+            do("mm1", b, v); do("evg", b, v, "V" if b == 7 and v % 2 else "S")
+            if b == 2 and v == 2: do("mm2", 0, 4); do("sig",0,4); do("qg",1,4); do("glu",0,4)
+            if b > 2 and v == 0: do("qg", b-1, 4); do("glu", b-1, 0);
+        if b < 7: do("il", b+1, 1, 2)
+        p = (b-1, 4)
+        do("mm2", *p); do("sig", *p)
+        if b < 7: do("qx", b+1)
+        for v in range(4, 8):
+            do("mm1", b, v); do("evg", b, v, "V" if b == 7 and v % 2 else "S")
+            if v == 4: do("qg", b, 0); do("glu", *p)
+            if v == 5 and b < 6: do("il", b+2, 0, 2)
+            if v == 6 and b == 2:
+                do("tro",0,0); do("tro",0,4); do("evo",0,0); do("evo",0,4)
+            if v == 5 and b == 7: do("qg", 7, 4)
+        if b < 7 or True:
+            do("mm2", b, 0); do("sig", b, 0)
+            do("tro", b-1, 0); do("tro", b-1, 4); do("evo", b-1, 0); do("evo", b-1, 4)
+    do("glu", 7, 0); do("qg", 7, 6); do("mm2",7,4); do("sig",7,4); do("glu",7,4); do("mm2",7,6); do("sig",7,6); do("glu",7,6)
+    do("tro",7,0); do("evo",7,0); do("tro",7,4); do("evo",7,4); do("tro",7,6); do("evo",7,6)
 
 
 def tile_stsgcm_pa_t_w8_kernel(tc, x, A_bytes, A_scale, W0_words, W0_scales, b0, out):
@@ -72,8 +83,11 @@ def tile_stsgcm_pa_t_w8_kernel(tc, x, A_bytes, A_scale, W0_words, W0_scales, b0,
         ident = const.tile([P, P], F32, name="ident")
         make_identity(nc, ident[:])
 
-        scale_bc = const.tile([P, NODES], F32, name="scale_bc")
-        nc.scalar.dma_start(out=scale_bc[:], in_=A_scale.rearrange("o k -> (o k)").partition_broadcast(P))
+        scale = const.tile([P, 2, 4], F32, name="scale")
+        bias = const.tile([P, 2], BF16, name="bias")
+        with nc.allow_non_contiguous_dma(reason="short rows: four scales, one bias value"):
+            nc.scalar.dma_start(out=scale[:], in_=A_scale.rearrange("o (g p t) -> (o p) g t", p=P, t=4))
+            nc.scalar.dma_start(out=bias[:], in_=b0.rearrange("(o p) -> p o", p=P))
 
         raw = {}
         a_raw = {}
@@ -89,21 +103,18 @@ def tile_stsgcm_pa_t_w8_kernel(tc, x, A_bytes, A_scale, W0_words, W0_scales, b0,
             for k in range(lo, hi):
                 a_raw[k] = t[:, k - lo, :]
 
-        load_x(0, 0)
         load_a(0, 2)
+        load_x(0, 0)
         load_x(0, 1)
-        load_a(2, 5)
+        load_a(2, 4)
         load_x(1, 0)
-        load_a(5, 8)
         load_x(1, 1)
+        load_a(4, 8)
         w_words = const.tile([P, 2 * HID], U32, name="w_words", align_bytes=64)
         nc.sync.dma_start(out=w_words[:].bitcast(I32), in_=W0_words.rearrange("o p n t -> (o p) (n t)").bitcast(I32))
         ws_view = W0_scales.rearrange("o q n -> (o q) n").bitcast(I32)
         for q in range(4):
             nc.sync.dma_start(out=w_scales[32 * q : 32 * q + 4, :].bitcast(I32), in_=ws_view[4 * q : 4 * q + 4, :])
-        bias = const.tile([P, 2], BF16, name="bias")
-        with nc.allow_non_contiguous_dma(reason="256 bias values, one to a partition and half"):
-            nc.sync.dma_start(out=bias[:], in_=b0.rearrange("(o p) -> p o", p=P))
         for b in range(2, 8):
             for g in range(2):
                 load_x(b, g)
@@ -116,7 +127,7 @@ def tile_stsgcm_pa_t_w8_kernel(tc, x, A_bytes, A_scale, W0_words, W0_scales, b0,
             lo, hi = (0, 512) if hf == 2 else (256 * hf, 256 * hf + 256)
             dst = xg[b][:, g, :].rearrange("p (t c) -> p t c", t=4)[:, :, lo:hi]
             src = raw[b, g][:, :, lo:hi]
-            eng = nc.scalar.copy if "%d %d %d" % (b, g, hf) in SCALAR_IL else nc.vector.tensor_copy
+            eng = nc.scalar.copy if (b, g, hf) in IL_SCALAR else nc.vector.tensor_copy
             eng(
                 out=dst.rearrange("p t (m i j) -> p m j i t", i=2, j=4),
                 in_=src.rearrange("p j (m i t) -> p m j i t", i=2, t=4),
@@ -132,9 +143,9 @@ def tile_stsgcm_pa_t_w8_kernel(tc, x, A_bytes, A_scale, W0_words, W0_scales, b0,
             )
             xq[b] = (codes, scales)
 
-        def prod(k):
+        def cast(k):
             aw[k] = work.tile([P, NODES], BF16, name="aw", bufs=4)
-            nc.vector.tensor_tensor(out=aw[k][:], in0=a_raw[k].bitcast(FP8), in1=scale_bc[:], op=MULT)
+            nc.scalar.copy(out=aw[k][:], in_=a_raw[k].bitcast(FP8))
 
         def tra(k):
             at[k] = pst.tile([P, 4, P], F32, name="pst_t")
@@ -145,10 +156,13 @@ def tile_stsgcm_pa_t_w8_kernel(tc, x, A_bytes, A_scale, W0_words, W0_scales, b0,
 
         def eva(k):
             ag = work.tile([P, NODES], BF16, name="ag", bufs=4, align_bytes=64)
-            nc.scalar.copy(
-                out=ag[:].bitcast(F32).rearrange("p (g v u) -> p g v u", g=2, u=2),
-                in_=at[k][:].rearrange("p (g u) v -> p g v u", g=2),
-            )
+            for g in range(2):
+                nc.vector.tensor_tensor(
+                    out=ag[:, 512 * g : 512 * (g + 1)].rearrange("p (v u e) -> p v u e", u=2, e=2),
+                    in0=at[k][:, 2 * g : 2 * g + 2, :].rearrange("p u v -> p (u v)").bitcast(BF16).rearrange("p (u v e) -> p v u e", u=2, e=2),
+                    in1=scale[:, g, :].rearrange("p (u e) -> p u e", u=2).unsqueeze(1).to_broadcast([P, P, 2, 2]),
+                    op=MULT,
+                )
             aq[k] = ag
 
         def qa(k):
@@ -175,57 +189,67 @@ def tile_stsgcm_pa_t_w8_kernel(tc, x, A_bytes, A_scale, W0_words, W0_scales, b0,
                         stop=(g == 1),
                     )
 
-        def evg(b, k):
-            h = (b, k // 4)
+        def evg(b, k, engine="S"):
+            h = (b, 4 * (k // 4))
             if k % 4 == 0:
                 gg[h] = work.tile([P, 4, P, 4], BF16, name="gg", bufs=4, align_bytes=64)
-            nc.scalar.copy(out=gg[h][:, k % 4, :, :], in_=acc[b, k][:].rearrange("p t v -> p v t"))
+            eng = nc.scalar.copy if engine == "S" else nc.vector.tensor_copy
+            eng(out=gg[h][:, k % 4, :, :], in_=acc[b, k][:].rearrange("p t v -> p v t"))
 
-        def qg(b, h):
+        def width(b, v0):
+            return 2 if (b, v0) in ((7, 4), (7, 6)) and SPLIT else 4
+
+        def qg(b, v0):
+            n = width(b, v0)
             codes = work.tile([P, 512], U32, name="gcodes", bufs=4, align_bytes=64)
             scales = work.tile([P, 512], U8, name="gscales", bufs=4, align_bytes=64)
+            src = gg[b, 4 * (v0 // 4)][:, v0 % 4 : v0 % 4 + n, :, :]
             nc.vector.quantize_mx(
-                out=codes[:].bitcast(FP8X4), scales=scales[:], in_=gg[b, h][:].rearrange("p k v t -> p (k v t)")
+                out=codes[:, : P * n].bitcast(FP8X4), scales=scales[:, : P * n], in_=src.rearrange("p k v t -> p (k v t)")
             )
-            gq[b, h] = (codes, scales)
+            gq[b, v0] = (codes, scales)
 
-        def mm2(b, h):
-            yv[b, h] = psy.tile([P, 512], F32, name="yv")
-            yg[b, h] = psy.tile([P, 512], F32, name="yg")
+        def mm2(b, v0):
+            n = width(b, v0) * P
+            yv[b, v0] = psy.tile([P, 512], F32, name="yv")
+            yg[b, v0] = psy.tile([P, 512], F32, name="yg")
             for dst, o in ((yg, 1), (yv, 0)):
                 nc.tensor.matmul_mx(
-                    out=dst[b, h][:],
+                    out=dst[b, v0][:, :n],
                     lhsT=w_words[:, HID * o : HID * (o + 1)].bitcast(FP8X4),
                     lhsT_scale=w_scales[:, HID * o : HID * (o + 1)],
-                    rhs=gq[b, h][0][:].bitcast(FP8X4),
-                    rhs_scale=gq[b, h][1][:],
+                    rhs=gq[b, v0][0][:, :n].bitcast(FP8X4),
+                    rhs_scale=gq[b, v0][1][:, :n],
                     start=True,
                     stop=True,
                 )
 
-        def sigm(b, h):
-            sig[b, h] = work.tile([P, 512], F32, name="sig")
-            nc.scalar.activation(out=sig[b, h][:], in_=yg[b, h][:], func=ACT.Sigmoid, bias=bias[:, 1:2])
+        def sigm(b, v0):
+            n = width(b, v0) * P
+            sig[b, v0] = work.tile([P, 512], F32, name="sig")
+            nc.scalar.activation(out=sig[b, v0][:, :n], in_=yg[b, v0][:, :n], func=ACT.Sigmoid, bias=bias[:, 1:2])
 
-        def glu(b, h):
-            hh[b, h] = work.tile([P, 512], F32, name="hh", bufs=7)
+        def glu(b, v0):
+            n = width(b, v0) * P
+            hh[b, v0] = work.tile([P, 512], F32, name="hh", bufs=6)
             nc.vector.scalar_tensor_tensor(
-                out=hh[b, h][:], in0=yv[b, h][:], scalar=bias[:, 0:1], in1=sig[b, h][:], op0=ADD, op1=MULT
+                out=hh[b, v0][:, :n], in0=yv[b, v0][:, :n], scalar=bias[:, 0:1], in1=sig[b, v0][:, :n], op0=ADD, op1=MULT
             )
 
-        def trout(b, h):
-            tro[b, h] = pst.tile([P, 4, P], F32, name="pst_t")
-            for k in range(4):
-                nc.tensor.transpose(tro[b, h][:, k, :], hh[b, h][:, P * k : P * (k + 1)], ident[:])
+        def trout(b, v0):
+            tro[b, v0] = pst.tile([P, 4, P], F32, name="pst_t")
+            for k in range(width(b, v0)):
+                nc.tensor.transpose(tro[b, v0][:, k, :], hh[b, v0][:, P * k : P * (k + 1)], ident[:])
 
-        def evo(b, h):
-            ob[b, h] = work.tile([P, 4, P], F32, name="ob", bufs=4)
-            eng = nc.scalar.copy if h == 0 else nc.vector.tensor_copy
-            eng(out=ob[b, h][:], in_=tro[b, h][:])
-            nc.sync.dma_start(out=out_view[b][:, 4 * h : 4 * h + 4, :], in_=ob[b, h][:])
+        def evo(b, v0, engine="S"):
+            n = width(b, v0)
+            ob[b, v0] = work.tile([P, 4, P], F32, name="ob", bufs=4)
+            eng = nc.scalar.copy if engine == "S" else nc.vector.tensor_copy
+            eng(out=ob[b, v0][:, :n, :], in_=tro[b, v0][:, :n, :])
+            nc.sync.dma_start(out=out_view[b][:, v0 : v0 + n, :], in_=ob[b, v0][:, :n, :])
 
         stages = {
-            "il": il, "qx": qx, "prod": prod, "tra": tra, "eva": eva, "qa": qa, "mm1": mm1, "evg": evg,
+            "il": il, "qx": qx, "cast": cast, "tra": tra, "eva": eva, "qa": qa, "mm1": mm1, "evg": evg,
             "qg": qg, "mm2": mm2, "sig": sigm, "glu": glu, "tro": trout, "evo": evo,
         }
 
@@ -233,7 +257,4 @@ def tile_stsgcm_pa_t_w8_kernel(tc, x, A_bytes, A_scale, W0_words, W0_scales, b0,
             stages[name](*args)
 
         with tc.manual_schedule():
-            for item in ORDER.split(", "):
-                if item:
-                    words = item.split(" ")
-                    do(words[0], *[int(w) for w in words[1:]])
+            program(do)

@@ -21,43 +21,49 @@ FLOPS = 2 * NODES * NODES * BATCH * CHAN + 2 * NODES * BATCH * CHAN * 2 * HID
 
 
 SPLIT = True
-IL_SCALAR = {(0,1,1),(1,0,0),(1,0,1),(2,0,0),(2,0,1)}
+IL_SCALAR = {(0, 1, 1), (1, 0, 0), (1, 0, 1), (2, 0, 0), (2, 0, 1)}
+HEAD = (
+    "cast 0, il 0 0 2, tra 0, cast 1, il 0 1 1, cast 2, il 0 1 0, eva 0, qx 0, cast 3, "
+    "tra 1, eva 1, tra 2, tra 3, eva 2, il 1 0 0, qa 0, qa 1, il 1 0 1, cast 4, "
+    "qa 2, eva 3, mm1 0 2, tra 4, cast 5, il 1 1 2, qa 3, tra 5, eva 4, evg 0 2, "
+    "mm1 0 0, mm1 0 1, cast 6, mm1 0 3, cast 7, evg 0 0, qx 1, tra 6, evg 0 1, eva 5, "
+    "mm1 1 3, evg 0 3, evg 1 3, tra 7, il 2 0 1, qa 4, eva 6, il 2 0 0, mm1 1 2, qg 0 0, "
+    "mm1 1 0, mm1 1 1, evg 1 2 V, evg 1 0, mm1 0 4, qa 5, qa 6, mm1 1 6, mm2 0 0, eva 7, "
+    "evg 1 1, il 2 1 2, mm1 1 4, evg 0 4, sig 0 0, evg 1 6, qa 7, mm1 0 6, qg 1 0, evg 1 4, "
+    "mm1 0 5, mm1 1 7, glu 0 0, mm1 0 7, evg 0 6, evg 0 5, qx 2, mm2 1 0, tro 0 0, evg 1 7, "
+    "evg 0 7, il 3 1 2, qg 0 4, sig 1 0, mm1 2 0, evo 0 0, mm1 2 1, mm1 1 5, mm1 2 2, evg 2 0, "
+    "glu 1 0, mm2 0 4, il 4 0 2, mm1 2 3, evg 1 5, evg 2 1, sig 0 4, qg 1 4, glu 0 4, mm1 2 4, "
+    "evg 2 2, evg 2 3, mm1 2 5, il 3 0 2, mm2 1 4, qg 2 0, evg 2 4, sig 1 4, tro 0 4, glu 1 4, "
+    "mm1 2 6, mm1 2 7, evo 0 4, evg 2 6, qx 3, tro 1 0, evg 2 7, tro 1 4, mm2 2 0, evo 1 0, "
+    "sig 2 0, evg 2 5 V, evo 1 4, "
+)
+STEADY = (
+    "qg -1 4, mm1 0 0, mm1 0 1, glu -1 0, evg 0 0 V, evg 0 1, mm1 0 2, mm1 0 3, il 1 1 2, mm2 -1 4, "
+    "mm1 0 4, evg 0 2, mm1 0 5, evg 0 3, sig -1 4, evg 0 4, qg 0 0, evg 0 5, mm1 0 6, mm1 0 7, "
+    "glu -1 4, evg 0 6, mm2 0 0, tro -1 0, tro -1 4, qx 1, evg 0 7, sig 0 0, il 2 0 2, evo -1 0, "
+    "evo -1 4, "
+)
+TAIL = (
+    "mm1 7 0, mm1 7 1, qg 6 4, mm1 7 2, glu 6 0, evg 7 0 V, mm2 6 4, evg 7 1, mm1 7 3, sig 6 4, "
+    "evg 7 2 V, glu 6 4, evg 7 3, qg 7 0, mm1 7 4, mm1 7 5, evg 7 5 V, mm1 7 6, evg 7 4, evg 7 6 V, "
+    "mm2 7 0, qg 7 4, tro 6 0, sig 7 0, tro 6 4, mm1 7 7, evo 6 0, evg 7 7, glu 7 0, mm2 7 4, "
+    "sig 7 4, qg 7 6, evo 6 4, glu 7 4, mm2 7 6, tro 7 4, sig 7 6, glu 7 6, tro 7 0, evo 7 0 V, "
+    "evo 7 4, tro 7 6, evo 7 6 V, "
+)
+
+
 def program(do):
-    def il(b, g):
-        if (b, g, 0) in IL_SCALAR:
-            do("il", b, g, 0); do("il", b, g, 1)
-        else:
-            do("il", b, g, 2)
-    do("cast", 0); do("tra", 0); do("cast", 1); do("tra", 1)
-    do("il", 0, 0, 2); do("il",0,1,1); do("eva", 0); do("cast",2); do("tra",2); do("eva", 1); do("cast",3); do("tra",3); do("il", 0, 1, 0); do("qx", 0)
-    do("eva", 2); do("il",1,0,0); do("il",1,0,1); do("eva", 3); do("qa",0); do("il", 1, 1, 2); do("qa",1); do("qa", 2); do("qx", 1); do("qa", 3)
-    do("cast",4); do("mm1",0,0); do("tra",4); do("cast",5); do("tra",5); do("il",2,0,0); do("eva",4); do("mm1",0,1); do("mm1",0,2); do("mm1",0,3)
-    do("evg",0,0); do("cast",6); do("evg",0,1); do("eva",5); do("cast",7); do("evg",0,2); do("evg",0,3); do("mm1",1,0); do("tra",6); do("tra",7); do("qa",4)
-    do("mm1",1,1); do("evg",1,0); do("il",2,0,1); do("qg",0,0); do("eva",6); do("evg",1,1); do("mm1",1,2); do("qa",5); do("evg",1,2); do("mm1",1,3); do("evg",1,3); do("eva",7); do("mm2",0,0); do("qa",6); do("sig",0,0)
-    do("qg",1,0); do("mm1",0,4); do("mm1",1,4); do("evg",0,4); do("glu",0,0); do("qa",7); do("evg",1,4); do("mm1",0,5); do("mm1",1,5); do("evg",0,5); do("il",2,1,2); do("evg",1,5)
-    do("mm2",1,0); do("sig",1,0); do("mm1",0,6); do("mm1",1,6); do("evg",0,6); do("glu",1,0); do("evg",1,6); do("mm1",0,7); do("mm1",1,7); do("qx",2); do("evg",0,7); do("evg",1,7)
-    do("qg",0,4); do("il",3,0,2)
-    for b in range(2, 8):
-        for v in range(4):
-            do("mm1", b, v); do("evg", b, v, "V" if b == 7 and v % 2 else "S")
-            if b == 2 and v == 2: do("mm2", 0, 4); do("sig",0,4); do("qg",1,4); do("glu",0,4)
-            if b > 2 and v == 0: do("qg", b-1, 4); do("glu", b-1, 0);
-        if b < 7: do("il", b+1, 1, 2)
-        p = (b-1, 4)
-        do("mm2", *p); do("sig", *p)
-        if b < 7: do("qx", b+1)
-        for v in range(4, 8):
-            do("mm1", b, v); do("evg", b, v, "V" if b == 7 and v % 2 else "S")
-            if v == 4: do("qg", b, 0); do("glu", *p)
-            if v == 5 and b < 6: do("il", b+2, 0, 2)
-            if v == 6 and b == 2:
-                do("tro",0,0); do("tro",0,4); do("evo",0,0); do("evo",0,4)
-            if v == 5 and b == 7: do("qg", 7, 4)
-        if b < 7 or True:
-            do("mm2", b, 0); do("sig", b, 0)
-            do("tro", b-1, 0); do("tro", b-1, 4); do("evo", b-1, 0); do("evo", b-1, 4)
-    do("glu", 7, 0); do("qg", 7, 6); do("mm2",7,4); do("sig",7,4); do("glu",7,4); do("mm2",7,6); do("sig",7,6); do("glu",7,6)
-    do("tro",7,0); do("evo",7,0); do("tro",7,4); do("evo",7,4); do("tro",7,6); do("evo",7,6)
+    for text, entries in ((HEAD, (0,)), (STEADY, range(3, 7)), (TAIL, (0,))):
+        for b in entries:
+            for item in text.split(", "):
+                if item:
+                    words = item.split(" ")
+                    engine = words.pop() if words[-1] == "V" else None
+                    args = [int(w) for w in words[1:]]
+                    args[0] += b
+                    if words[0] in ("il", "qx") and args[0] > 7:
+                        continue
+                    do(words[0], *(args + [engine] if engine else args))
 
 
 def tile_stsgcm_pa_t_w8_kernel(tc, x, A_bytes, A_scale, W0_words, W0_scales, b0, out):
@@ -191,7 +197,7 @@ def tile_stsgcm_pa_t_w8_kernel(tc, x, A_bytes, A_scale, W0_words, W0_scales, b0,
 
         def evg(b, k, engine="S"):
             h = (b, 4 * (k // 4))
-            if k % 4 == 0:
+            if h not in gg:
                 gg[h] = work.tile([P, 4, P, 4], BF16, name="gg", bufs=4, align_bytes=64)
             eng = nc.scalar.copy if engine == "S" else nc.vector.tensor_copy
             eng(out=gg[h][:, k % 4, :, :], in_=acc[b, k][:].rearrange("p t v -> p v t"))

from contextlib import ExitStack

import concourse.mybir as mybir
from concourse.masks import make_identity

F32 = mybir.dt.float32
BF16 = mybir.dt.bfloat16
I32 = mybir.dt.int32
U32 = mybir.dt.uint32
U8 = mybir.dt.uint8
FP8 = mybir.dt.float8_e4m3fn
FP8X4 = mybir.dt.float8_e4m3fn_x4
MULT = mybir.AluOpType.mult
ADD = mybir.AluOpType.add
ACT = mybir.ActivationFunctionType

NODES, BATCH, CHAN, HID = 1024, 8, 512, 128
P = 128
VT = NODES // P
FLOPS = 2 * NODES * NODES * BATCH * CHAN + 2 * NODES * BATCH * CHAN * 2 * HID


SPLIT = True
IL_SCALAR = {(0, 1, 1), (1, 0, 0), (1, 0, 1), (2, 0, 0), (2, 0, 1)}
HEAD = (
    "cast 0, il 0 0 2, tra 0, cast 1, il 0 1 1, cast 2, il 0 1 0, eva 0, qx 0, cast 3, "
    "tra 1, eva 1, tra 2, tra 3, eva 2, il 1 0 0, qa 0, qa 1, il 1 0 1, cast 4, "
    "qa 2, eva 3, mm1 0 2, tra 4, cast 5, il 1 1 2, qa 3, tra 5, eva 4, evg 0 2, "
    "mm1 0 0, mm1 0 1, cast 6, mm1 0 3, cast 7, evg 0 0, qx 1, tra 6, evg 0 1, eva 5, "
    "mm1 1 3, evg 0 3, evg 1 3, tra 7, il 2 0 1, qa 4, eva 6, il 2 0 0, mm1 1 2, qg 0 0, "
    "mm1 1 0, mm1 1 1, evg 1 2 V, evg 1 0, mm1 0 4, qa 5, qa 6, mm1 1 6, mm2 0 0, eva 7, "
    "evg 1 1, il 2 1 2, mm1 1 4, evg 0 4, sig 0 0, evg 1 6, qa 7, mm1 0 6, qg 1 0, evg 1 4, "
    "mm1 0 5, mm1 1 7, glu 0 0, mm1 0 7, evg 0 6, evg 0 5, qx 2, mm2 1 0, tro 0 0, evg 1 7, "
    "evg 0 7, il 3 1 2, qg 0 4, sig 1 0, mm1 2 0, evo 0 0, mm1 2 1, mm1 1 5, mm1 2 2, evg 2 0, "
    "glu 1 0, mm2 0 4, il 4 0 2, mm1 2 3, evg 1 5, evg 2 1, sig 0 4, qg 1 4, glu 0 4, mm1 2 4, "
    "evg 2 2, evg 2 3, mm1 2 5, il 3 0 2, mm2 1 4, qg 2 0, evg 2 4, sig 1 4, tro 0 4, glu 1 4, "
    "mm1 2 6, mm1 2 7, evo 0 4, evg 2 6, qx 3, tro 1 0, evg 2 7, tro 1 4, mm2 2 0, evo 1 0, "
    "sig 2 0, evg 2 5 V, evo 1 4, "
)
STEADY = (
    "qg -1 4, mm1 0 0, mm1 0 1, glu -1 0, evg 0 0 V, evg 0 1, mm1 0 2, mm1 0 3, il 1 1 2, mm2 -1 4, "
    "mm1 0 4, evg 0 2, mm1 0 5, evg 0 3, sig -1 4, evg 0 4, qg 0 0, evg 0 5, mm1 0 6, mm1 0 7, "
    "glu -1 4, evg 0 6, mm2 0 0, tro -1 0, tro -1 4, qx 1, evg 0 7, sig 0 0, il 2 0 2, evo -1 0, "
    "evo -1 4, "
)
TAIL = (
    "mm1 7 0, mm1 7 1, qg 6 4, mm1 7 2, glu 6 0, evg 7 0 V, mm2 6 4, evg 7 1, mm1 7 3, sig 6 4, "
    "evg 7 2 V, glu 6 4, evg 7 3, qg 7 0, mm1 7 4, mm1 7 5, evg 7 5 V, mm1 7 6, evg 7 4, evg 7 6 V, "
    "mm2 7 0, qg 7 4, tro 6 0, sig 7 0, tro 6 4, mm1 7 7, evo 6 0, evg 7 7, glu 7 0, mm2 7 4, "
    "sig 7 4, qg 7 6, evo 6 4, glu 7 4, mm2 7 6, tro 7 4, sig 7 6, glu 7 6, tro 7 0, evo 7 0 V, "
    "evo 7 4, tro 7 6, evo 7 6 V, "
)


def program(do):
    for text, entries in ((HEAD, (0,)), (STEADY, range(3, 7)), (TAIL, (0,))):
        for b in entries:
            for item in text.split(", "):
                if item:
                    words = item.split(" ")
                    engine = words.pop() if words[-1] == "V" else None
                    args = [int(w) for w in words[1:]]
                    args[0] += b
                    if words[0] in ("il", "qx") and args[0] > 7:
                        continue
                    do(words[0], *(args + [engine] if engine else args))


def tile_stsgcm_pa_t_w8_kernel(tc, x, A_bytes, A_scale, W0_words, W0_scales, b0, out):
    nc = tc.nc
    with ExitStack() as ctx:
        const = ctx.enter_context(tc.tile_pool(name="const", bufs=1))
        raws = ctx.enter_context(tc.tile_pool(name="raws", bufs=1))
        work = ctx.enter_context(tc.tile_pool(name="work", bufs=3))
        psg = ctx.enter_context(tc.psum_pool(name="psg", bufs=4))
        pst = ctx.enter_context(tc.psum_pool(name="pst", bufs=2))
        psy = ctx.enter_context(tc.psum_pool(name="psy", bufs=1))

        x_view = x.rearrange("(g p j) b c -> g b p j c", p=P, j=4)
        a_view = A_bytes.rearrange("(k p) w -> p k w", p=P)
        out_view = out.rearrange("(k p) b j -> b p k j", p=P)

        warm = const.tile([P, 1], F32, name="warm")
        nc.vector.memset(warm[:], 0.0)
        nc.scalar.activation(out=warm[:], in_=warm[:], func=ACT.Sigmoid)
        w_scales = const.tile([P, 2 * HID], U8, name="w_scales", align_bytes=64)
        nc.vector.memset(w_scales[:].bitcast(I32), 0)

        ident = const.tile([P, P], F32, name="ident")
        make_identity(nc, ident[:])

        scale = const.tile([P, 2, 4], F32, name="scale")
        bias = const.tile([P, 2], BF16, name="bias")
        with nc.allow_non_contiguous_dma(reason="short rows: four scales, one bias value"):
            nc.scalar.dma_start(out=scale[:], in_=A_scale.rearrange("o (g p t) -> (o p) g t", p=P, t=4))
            nc.scalar.dma_start(out=bias[:], in_=b0.rearrange("(o p) -> p o", p=P))

        raw = {}
        a_raw = {}

        def load_x(b, g):
            t = raws.tile([P, 4, CHAN], BF16, name="raw%d_%d" % (b, g))
            nc.sync.dma_start(out=t[:], in_=x_view[g][b])
            raw[b, g] = t

        def load_a(lo, hi):
            t = raws.tile([P, hi - lo, NODES], U8, name="abytes%d" % lo)
            nc.sync.dma_start(out=t[:], in_=a_view[:, lo:hi, :])
            for k in range(lo, hi):
                a_raw[k] = t[:, k - lo, :]

        load_a(0, 2)
        load_x(0, 0)
        load_x(0, 1)
        load_a(2, 4)
        load_x(1, 0)
        load_x(1, 1)
        load_a(4, 8)
        w_words = const.tile([P, 2 * HID], U32, name="w_words", align_bytes=64)
        nc.sync.dma_start(out=w_words[:].bitcast(I32), in_=W0_words.rearrange("o p n t -> (o p) (n t)").bitcast(I32))
        ws_view = W0_scales.rearrange("o q n -> (o q) n").bitcast(I32)
        for q in range(4):
            nc.sync.dma_start(out=w_scales[32 * q : 32 * q + 4, :].bitcast(I32), in_=ws_view[4 * q : 4 * q + 4, :])
        for b in range(2, 8):
            for g in range(2):
                load_x(b, g)

        xq, aw, at, aq, xg, acc, gg, gq, yv, yg, sig, hh, tro, ob = ({} for _ in range(14))

        def il(b, g, hf):
            if b not in xg:
                xg[b] = work.tile([P, 2, 2048], BF16, name="xg", bufs=3, align_bytes=64)
            lo, hi = (0, 512) if hf == 2 else (256 * hf, 256 * hf + 256)
            dst = xg[b][:, g, :].rearrange("p (t c) -> p t c", t=4)[:, :, lo:hi]
            src = raw[b, g][:, :, lo:hi]
            eng = nc.scalar.copy if (b, g, hf) in IL_SCALAR else nc.vector.tensor_copy
            eng(
                out=dst.rearrange("p t (m i j) -> p m j i t", i=2, j=4),
                in_=src.rearrange("p j (m i t) -> p m j i t", i=2, t=4),
            )

        def qx(b):
            codes = work.tile([P, 2, CHAN], U32, name="xcodes", bufs=4, align_bytes=64)
            scales = work.tile([P, 2, CHAN], U8, name="xscales", bufs=4, align_bytes=64)
            nc.vector.quantize_mx(
                out=codes[:].rearrange("p g c -> p (g c)").bitcast(FP8X4),
                scales=scales[:].rearrange("p g c -> p (g c)"),
                in_=xg[b][:].rearrange("p g c -> p (g c)"),
            )
            xq[b] = (codes, scales)

        def cast(k):
            aw[k] = work.tile([P, NODES], BF16, name="aw", bufs=4)
            nc.scalar.copy(out=aw[k][:], in_=a_raw[k].bitcast(FP8))

        def tra(k):
            at[k] = pst.tile([P, 4, P], F32, name="pst_t")
            words = aw[k][:].bitcast(F32)
            for g in range(2):
                for u in range(2):
                    nc.tensor.transpose(at[k][:, 2 * g + u, :], words[:, 256 * g + u : 256 * (g + 1) : 2], ident[:])

        def eva(k):
            ag = work.tile([P, NODES], BF16, name="ag", bufs=4, align_bytes=64)
            for g in range(2):
                nc.vector.tensor_tensor(
                    out=ag[:, 512 * g : 512 * (g + 1)].rearrange("p (v u e) -> p v u e", u=2, e=2),
                    in0=at[k][:, 2 * g : 2 * g + 2, :].rearrange("p u v -> p (u v)").bitcast(BF16).rearrange("p (u v e) -> p v u e", u=2, e=2),
                    in1=scale[:, g, :].rearrange("p (u e) -> p u e", u=2).unsqueeze(1).to_broadcast([P, P, 2, 2]),
                    op=MULT,
                )
            aq[k] = ag

        def qa(k):
            codes = const.tile([P, 2, P], U32, name="acodes%d" % k, align_bytes=64)
            scales = const.tile([P, 2, P], U8, name="ascales%d" % k, align_bytes=64)
            nc.vector.quantize_mx(
                out=codes[:].rearrange("p g v -> p (g v)").bitcast(FP8X4),
                scales=scales[:].rearrange("p g v -> p (g v)"),
                in_=aq[k][:],
            )
            aq[k] = (codes, scales)

        def mm1(b, k):
            acc[b, k] = psg.tile([P, 4, P], F32, name="psg_t")
            for t in range(4):
                for g in range(2):
                    nc.tensor.matmul_mx(
                        out=acc[b, k][:, t, :],
                        lhsT=xq[b][0][:, g, P * t : P * (t + 1)].bitcast(FP8X4),
                        lhsT_scale=xq[b][1][:, g, P * t : P * (t + 1)],
                        rhs=aq[k][0][:, g, :].bitcast(FP8X4),
                        rhs_scale=aq[k][1][:, g, :],
                        start=(g == 0),
                        stop=(g == 1),
                    )

        def evg(b, k, engine="S"):
            h = (b, 4 * (k // 4))
            if h not in gg:
                gg[h] = work.tile([P, 4, P, 4], BF16, name="gg", bufs=4, align_bytes=64)
            eng = nc.scalar.copy if engine == "S" else nc.vector.tensor_copy
            eng(out=gg[h][:, k % 4, :, :], in_=acc[b, k][:].rearrange("p t v -> p v t"))

        def width(b, v0):
            return 2 if (b, v0) in ((7, 4), (7, 6)) and SPLIT else 4

        def qg(b, v0):
            n = width(b, v0)
            codes = work.tile([P, 512], U32, name="gcodes", bufs=4, align_bytes=64)
            scales = work.tile([P, 512], U8, name="gscales", bufs=4, align_bytes=64)
            src = gg[b, 4 * (v0 // 4)][:, v0 % 4 : v0 % 4 + n, :, :]
            nc.vector.quantize_mx(
                out=codes[:, : P * n].bitcast(FP8X4), scales=scales[:, : P * n], in_=src.rearrange("p k v t -> p (k v t)")
            )
            gq[b, v0] = (codes, scales)

        def mm2(b, v0):
            n = width(b, v0) * P
            yv[b, v0] = psy.tile([P, 512], F32, name="yv")
            yg[b, v0] = psy.tile([P, 512], F32, name="yg")
            for dst, o in ((yg, 1), (yv, 0)):
                nc.tensor.matmul_mx(
                    out=dst[b, v0][:, :n],
                    lhsT=w_words[:, HID * o : HID * (o + 1)].bitcast(FP8X4),
                    lhsT_scale=w_scales[:, HID * o : HID * (o + 1)],
                    rhs=gq[b, v0][0][:, :n].bitcast(FP8X4),
                    rhs_scale=gq[b, v0][1][:, :n],
                    start=True,
                    stop=True,
                )

        def sigm(b, v0):
            n = width(b, v0) * P
            sig[b, v0] = work.tile([P, 512], F32, name="sig")
            nc.scalar.activation(out=sig[b, v0][:, :n], in_=yg[b, v0][:, :n], func=ACT.Sigmoid, bias=bias[:, 1:2])

        def glu(b, v0):
            n = width(b, v0) * P
            hh[b, v0] = work.tile([P, 512], F32, name="hh", bufs=6)
            nc.vector.scalar_tensor_tensor(
                out=hh[b, v0][:, :n], in0=yv[b, v0][:, :n], scalar=bias[:, 0:1], in1=sig[b, v0][:, :n], op0=ADD, op1=MULT
            )

        def trout(b, v0):
            tro[b, v0] = pst.tile([P, 4, P], F32, name="pst_t")
            for k in range(width(b, v0)):
                nc.tensor.transpose(tro[b, v0][:, k, :], hh[b, v0][:, P * k : P * (k + 1)], ident[:])

        def evo(b, v0, engine="S"):
            n = width(b, v0)
            ob[b, v0] = work.tile([P, 4, P], F32, name="ob", bufs=4)
            eng = nc.scalar.copy if engine == "S" else nc.vector.tensor_copy
            eng(out=ob[b, v0][:, :n, :], in_=tro[b, v0][:, :n, :])
            nc.sync.dma_start(out=out_view[b][:, v0 : v0 + n, :], in_=ob[b, v0][:, :n, :])

        stages = {
            "il": il, "qx": qx, "cast": cast, "tra": tra, "eva": eva, "qa": qa, "mm1": mm1, "evg": evg,
            "qg": qg, "mm2": mm2, "sig": sigm, "glu": glu, "tro": trout, "evo": evo,
        }

        def do(name, *args):
            stages[name](*args)

        with tc.manual_schedule():
            program(do)
